import numpy as np
import ml_dtypes


def mxq(x, axis, fmt="e4m3"):
    dtype, down = {"e4m3": (ml_dtypes.float8_e4m3fn, 7), "e5m2": (ml_dtypes.float8_e5m2, 14)}[fmt]
    v = np.moveaxis(np.asarray(x, np.float32).astype(ml_dtypes.bfloat16).astype(np.float64), axis, -1)
    blocks = v.reshape(v.shape[:-1] + (-1, 32))
    amax = np.abs(blocks).max(-1, keepdims=True)
    byte = np.maximum(np.where(amax > 0, np.frexp(amax)[1] - 1 + 127, 0) - down, 1)
    scale = np.exp2(byte - 127.0)
    codes = (blocks / scale).astype(np.float32).astype(dtype).astype(np.float64)
    return np.moveaxis((codes * scale).reshape(v.shape), -1, axis)


WIDE = False


def mx_kscale(k):
    if not WIDE:
        return np.ones(k)
    levels = np.array([10, -10, 5, -5, 0])
    a = np.random.permutation(np.resize(levels, k // 512 * 4)).reshape(k // 512, 4)
    idx = np.arange(k)
    return np.exp2(a[idx // 512, idx % 128 // 32])


BF16 = ml_dtypes.bfloat16


def bf(x):
    return np.asarray(x, np.float32).astype(BF16)


def f64(x):
    return np.asarray(x).astype(np.float64)


B, C, CI, N = 2, 1024, 512, 1024
EPS = 1e-5


def setup_inputs():
    s, t = mx_kscale(N), mx_kscale(CI)
    r = np.random.standard_normal
    return {"affinity": bf(r((B, N, N)) * 0.2 * s[None, None, :]),
            "g_x": bf(r((B, N, CI)) / s[None, :, None] * t[None, None, :]),
            "w_w": bf(r((C, CI)) * 1.5 / (0.2 * np.sqrt(N) * np.sqrt(CI)) / t[None, :]),
            "w_b": bf(r(C) * 0.3),
            "bn_gamma": bf(r(C)),
            "bn_beta": bf(r(C) * 0.5),
            "bn_mean": bf(r(C) * 0.5),
            "bn_var": bf(np.random.uniform(0.5, 1.5, C)),
            "x": bf(r((B, C, N)))}


def reference(affinity, g_x, w_w, w_b, bn_gamma, bn_beta, bn_mean, bn_var, x):
    y = (mxq(f64(affinity), 2, "e4m3") @ mxq(f64(g_x), 1, "e4m3")).transpose(0, 2, 1)
    wy = (mxq(f64(w_w), 1, "e4m3") @ mxq(y, 1, "e4m3")) + f64(w_b)[None, :, None]
    inv_std = 1.0 / np.sqrt(f64(bn_var) + EPS)
    wy = f64(bn_gamma)[None, :, None] * (wy - f64(bn_mean)[None, :, None]) * inv_std[None, :, None] + f64(bn_beta)[None, :, None]
    return wy + f64(x)

@@ -1,0 +1,289 @@
+from contextlib import ExitStack
+
+import concourse.masks as masks
+import concourse.mybir as mybir
+
+F32 = mybir.dt.float32
+BF16 = mybir.dt.bfloat16
+U32 = mybir.dt.uint32
+U8 = mybir.dt.uint8
+FP8X4 = mybir.dt.float8_e4m3fn_x4
+ALU = mybir.AluOpType
+
+P = 128
+PACK = 4
+K_PASS = P * PACK
+
+BATCH = 2
+POINTS = 1024
+INNER = 512
+CHANNELS = 1024
+EPS = 1e-5
+
+SOURCE_PASSES = POINTS // K_PASS
+INNER_TILES = INNER // P
+CHANNEL_TILES = CHANNELS // P
+CHUNK = 2 * P
+CHUNKS = POINTS // CHUNK
+HALF = 512
+HALVES = POINTS // HALF
+
+FLOPS = 2 * BATCH * POINTS * POINTS * INNER + 2 * BATCH * CHANNELS * INNER * POINTS
+
+
+def tile_sgcam_pb_kernel(
+    tc, affinity, g_x, w_w, w_b, bn_gamma, bn_beta, bn_mean, bn_var, x, out
+):
+    nc = tc.nc
+    with ExitStack() as ctx:
+        const = ctx.enter_context(tc.tile_pool(name="const", bufs=1))
+        loads = ctx.enter_context(tc.tile_pool(name="loads", bufs=1))
+        keep = ctx.enter_context(tc.tile_pool(name="keep", bufs=1))
+        stage = ctx.enter_context(tc.tile_pool(name="stage", bufs=2))
+        chunk_pool = ctx.enter_context(tc.tile_pool(name="chunk", bufs=4))
+        banks = ctx.enter_context(tc.psum_pool(name="banks", bufs=8))
+        ctx.enter_context(tc.manual_schedule())
+
+        def load_values(b, g):
+            raw = loads.tile([P, PACK, INNER], BF16, name="gx_raw%d%d" % (b, g))
+            nc.sync.dma_start(
+                out=raw[:].rearrange("q (u e) c -> q u (e c)", e=2),
+                in_=g_x[b, g * K_PASS : (g + 1) * K_PASS, :].rearrange("(u q e) c -> q u (e c)", u=2, e=2),
+            )
+            return raw
+
+        def load_affinity(b, i):
+            rows = loads.tile([P, 2, POINTS], BF16, name="aff%d%d" % (b, i))
+            nc.sync.dma_start(
+                out=rows[:],
+                in_=affinity[b, i * CHUNK : (i + 1) * CHUNK, :].rearrange("(p j) m -> p j m", j=2),
+            )
+            return rows
+
+        def load_residual(b, h):
+            rows = loads.tile([P, CHANNEL_TILES // 2, POINTS], BF16, name="x%d%d" % (b, h))
+            half_rows = slice(h * CHANNEL_TILES // 2, (h + 1) * CHANNEL_TILES // 2)
+            nc.sync.dma_start(out=rows[:], in_=x[b].rearrange("(p r) n -> p r n", r=CHANNEL_TILES)[:, half_rows, :])
+            return rows
+
+        def load_vector(vec, name):
+            rows = const.tile([P, CHANNEL_TILES], BF16, name=name)
+            nc.scalar.dma_start(out=rows[:], in_=vec.rearrange("(p r) -> p r", r=CHANNEL_TILES))
+            return rows
+
+        var_bf = load_vector(bn_var, "var_bf")
+        gamma_bf = load_vector(bn_gamma, "gamma_bf")
+        bias_bf = load_vector(w_b, "bias_bf")
+        mean_bf = load_vector(bn_mean, "mean_bf")
+        beta_bf = load_vector(bn_beta, "beta_bf")
+
+        gx_raw = {}
+        aff = {}
+        x_rows = {}
+        for g in range(SOURCE_PASSES):
+            gx_raw[0, g] = load_values(0, g)
+        for i in range(CHUNKS):
+            aff[0, i] = load_affinity(0, i)
+        w_rows = loads.tile([P, CHANNEL_TILES, INNER], BF16)
+        nc.sync.dma_start(out=w_rows[:], in_=w_w.rearrange("(p r) k -> p r k", r=CHANNEL_TILES))
+        for g in range(SOURCE_PASSES):
+            gx_raw[1, g] = load_values(1, g)
+        for h in range(2):
+            x_rows[0, h] = load_residual(0, h)
+        for i in range(CHUNKS):
+            aff[1, i] = load_affinity(1, i)
+        for h in range(2):
+            x_rows[1, h] = load_residual(1, h)
+
+        ident_f32 = const.tile([P, P], F32)
+        masks.make_identity(nc, ident_f32[:])
+        ident_bf = const.tile([P, P], BF16)
+        masks.make_identity(nc, ident_bf[:])
+
+        gx_grouped = {}
+        gx_codes = {}
+        gx_scales = {}
+
+        def regroup_values(b, g):
+            grouped = stage.tile([P, INNER, PACK], BF16, name="gx_grouped", align_bytes=64)
+            regroup = nc.vector.tensor_copy if g == 0 else nc.scalar.copy
+            regroup(
+                out=grouped[:].rearrange("q (c i) t -> q c t i", i=4),
+                in_=gx_raw[b, g][:].rearrange("q t (c i) -> q c t i", i=4),
+            )
+            gx_grouped[b, g] = grouped
+
+        def quantise_values(b, g):
+            codes = keep.tile([P, INNER], U32, name="gx_codes%d%d" % (b, g), align_bytes=64)
+            scales = keep.tile([P, INNER], U8, name="gx_scales%d%d" % (b, g), align_bytes=64)
+            nc.vector.quantize_mx(
+                out=codes[:].bitcast(FP8X4), scales=scales[:], in_=gx_grouped[b, g][:].rearrange("q c t -> q (c t)")
+            )
+            gx_codes[b, g] = codes
+            gx_scales[b, g] = scales
+
+        aff_grouped = {}
+        aff_codes = {}
+        aff_scales = {}
+
+        def flip_affinity(b, i):
+            words = aff[b, i][:].rearrange("p j m -> p (j m)").bitcast(F32)
+            grouped = chunk_pool.tile([P, SOURCE_PASSES * CHUNK * PACK], BF16, name="aff_grouped", align_bytes=64)
+            grouped_words = grouped[:].bitcast(F32).rearrange(
+                "q (g p j u) -> q g p j u", g=SOURCE_PASSES, j=2, u=2
+            )
+            for g in range(SOURCE_PASSES):
+                flipped = banks.tile([P, 2, 2, P], F32, name="flipped", tag="bank")
+                for j in range(2):
+                    for u in range(2):
+                        first = j * (POINTS // 2) + g * (K_PASS // 2) + u * P
+                        nc.tensor.transpose(flipped[:, j, u, :], words[:, first : first + P], ident_f32[:])
+                nc.scalar.copy(out=grouped_words[:, g], in_=flipped[:].rearrange("q j u p -> q p j u"))
+            aff_grouped[b, i] = grouped
+
+        def quantise_affinity(b, i):
+            codes = chunk_pool.tile([P, SOURCE_PASSES * CHUNK], U32, name="aff_codes", align_bytes=64)
+            scales = chunk_pool.tile([P, SOURCE_PASSES * CHUNK], U8, name="aff_scales", align_bytes=64)
+            nc.vector.quantize_mx(out=codes[:].bitcast(FP8X4), scales=scales[:], in_=aff_grouped[b, i][:])
+            aff_codes[b, i] = codes
+            aff_scales[b, i] = scales
+
+        y_grouped = {}
+        y_codes = {}
+        y_scales = {}
+
+        def aggregate(b, i):
+            h, k = divmod(i, HALF // CHUNK)
+            if k == 0:
+                y_grouped[b, h] = stage.tile([P, HALF, PACK], BF16, name="y_grouped", align_bytes=64)
+            for s in range(CHUNK // P):
+                y_bank = banks.tile([P, INNER_TILES, P], F32, name="y_bank", tag="bank")
+                for t in range(INNER_TILES):
+                    for g in range(SOURCE_PASSES):
+                        ci = slice(t * P, (t + 1) * P)
+                        pts = slice(g * CHUNK + s * P, g * CHUNK + (s + 1) * P)
+                        nc.tensor.matmul_mx(
+                            out=y_bank[:, t, :],
+                            lhsT=gx_codes[b, g][:, ci].bitcast(FP8X4),
+                            lhsT_scale=gx_scales[b, g][:, ci],
+                            rhs=aff_codes[b, i][:, pts].bitcast(FP8X4),
+                            rhs_scale=aff_scales[b, i][:, pts],
+                            start=(g == 0),
+                            stop=(g == SOURCE_PASSES - 1),
+                        )
+                lo = k * CHUNK + s * P
+                nc.scalar.copy(out=y_grouped[b, h][:, lo : lo + P, :], in_=y_bank[:].rearrange("q t n -> q n t"))
+
+        def quantise_y(b, h):
+            codes = keep.tile([P, HALF], U32, name="y_codes%d%d" % (b, h), align_bytes=64)
+            scales = keep.tile([P, HALF], U8, name="y_scales%d%d" % (b, h), align_bytes=64)
+            nc.vector.quantize_mx(
+                out=codes[:].bitcast(FP8X4), scales=scales[:], in_=y_grouped[b, h][:].rearrange("q n t -> q (n t)")
+            )
+            y_codes[b, h] = codes
+            y_scales[b, h] = scales
+
+        w_grouped = keep.tile([P, CHANNEL_TILES, P, PACK], BF16, align_bytes=64)
+        w_codes = keep.tile([P, CHANNELS], U32, align_bytes=64)
+        w_scales = keep.tile([P, CHANNELS], U8, align_bytes=64)
+
+        def flip_weights(pair):
+            flipped = banks.tile([P, 2, INNER_TILES, P], BF16, name="w_flipped", tag="bank")
+            for k in range(2):
+                for t in range(INNER_TILES):
+                    nc.tensor.transpose(flipped[:, k, t, :], w_rows[:, 2 * pair + k, t * P : (t + 1) * P], ident_bf[:])
+            copy_out = nc.scalar.copy if pair % 2 == 0 else nc.vector.tensor_copy
+            copy_out(out=w_grouped[:, 2 * pair : 2 * pair + 2, :, :], in_=flipped[:].rearrange("q k t p -> q k p t"))
+
+        def quantise_weights():
+            nc.vector.quantize_mx(
+                out=w_codes[:].bitcast(FP8X4), scales=w_scales[:], in_=w_grouped[:].rearrange("q r p t -> q (r p t)")
+            )
+
+        std = const.tile([P, CHANNEL_TILES], F32)
+        gain = const.tile([P, CHANNEL_TILES], F32)
+        shift = const.tile([P, CHANNEL_TILES], F32)
+
+        def start_batch_norm():
+            nc.vector.tensor_scalar_add(out=std[:], in0=var_bf[:], scalar1=EPS)
+            nc.scalar.sqrt(out=std[:], in_=std[:])
+
+        def finish_batch_norm():
+            nc.vector.reciprocal(out=gain[:], in_=std[:])
+            nc.vector.tensor_mul(out=gain[:], in0=gain[:], in1=gamma_bf[:])
+            nc.vector.tensor_sub(out=shift[:], in0=bias_bf[:], in1=mean_bf[:])
+            nc.vector.tensor_mul(out=shift[:], in0=shift[:], in1=gain[:])
+            nc.vector.tensor_add(out=shift[:], in0=shift[:], in1=beta_bf[:])
+
+        results = {}
+
+        def shift_residual(b, r):
+            result = keep.tile([P, POINTS], F32, name="result%d%d" % (b, r))
+            nc.gpsimd.tensor_scalar(
+                out=result[:],
+                in0=x_rows[b, r // (CHANNEL_TILES // 2)][:, r % (CHANNEL_TILES // 2), :],
+                scalar1=1.0,
+                scalar2=shift[:, r : r + 1],
+                op0=ALU.mult,
+                op1=ALU.add,
+            )
+            results[b, r] = result
+
+        def project(b, r):
+            chans = slice(r * P, (r + 1) * P)
+            result = results[b, r]
+            for h in range(HALVES):
+                acc = banks.tile([P, HALF], F32, name="acc", tag="bank")
+                nc.tensor.matmul_mx(
+                    out=acc[:],
+                    lhsT=w_codes[:, chans].bitcast(FP8X4),
+                    lhsT_scale=w_scales[:, chans],
+                    rhs=y_codes[b, h][:].bitcast(FP8X4),
+                    rhs_scale=y_scales[b, h][:],
+                    start=True,
+                    stop=True,
+                )
+                pts = slice(h * HALF, (h + 1) * HALF)
+                nc.vector.scalar_tensor_tensor(
+                    out=result[:, pts],
+                    in0=acc[:],
+                    scalar=gain[:, r : r + 1],
+                    in1=result[:, pts],
+                    op0=ALU.mult,
+                    op1=ALU.add,
+                )
+            nc.sync.dma_start(out=out[b].rearrange("(p r) n -> p r n", r=CHANNEL_TILES)[:, r, :], in_=result[:])
+
+        AHEAD = 2
+        start_batch_norm()
+        for b in range(BATCH):
+            for g in range(SOURCE_PASSES):
+                regroup_values(b, g)
+            if b == 0:
+                finish_batch_norm()
+            else:
+                quantise_y(b - 1, HALVES - 1)
+            for g in range(SOURCE_PASSES):
+                quantise_values(b, g)
+            for i in range(AHEAD):
+                flip_affinity(b, i)
+            for i in range(CHUNKS):
+                quantise_affinity(b, i)
+                if b > 0:
+                    project(b - 1, 2 * i)
+                    project(b - 1, 2 * i + 1)
+                if i + AHEAD < CHUNKS:
+                    flip_affinity(b, i + AHEAD)
+                elif b == 0:
+                    flip_weights(2 * (i + AHEAD - CHUNKS))
+                    flip_weights(2 * (i + AHEAD - CHUNKS) + 1)
+                aggregate(b, i)
+                if i == CHUNKS - 2:
+                    quantise_y(b, 0)
+            for r in range(CHANNEL_TILES):
+                shift_residual(b, r)
+            if b == 0:
+                quantise_weights()
+        quantise_y(BATCH - 1, HALVES - 1)
+        for r in range(CHANNEL_TILES):
+            project(BATCH - 1, r)

@@ -9,6 +9,7 @@ U32 = mybir.dt.uint32
 U8 = mybir.dt.uint8
 FP8X4 = mybir.dt.float8_e4m3fn_x4
 ALU = mybir.AluOpType
+ACT = mybir.ActivationFunctionType
 
 P = 128
 PACK = 4
@@ -219,14 +220,13 @@ def tile_sgcam_pb_kernel(
 
         def shift_residual(b, r):
             result = keep.tile([P, POINTS], F32, name="result%d%d" % (b, r))
-            nc.gpsimd.tensor_scalar(
-                out=result[:],
-                in0=x_rows[b, r // (CHANNEL_TILES // 2)][:, r % (CHANNEL_TILES // 2), :],
-                scalar1=1.0,
-                scalar2=shift[:, r : r + 1],
-                op0=ALU.mult,
-                op1=ALU.add,
-            )
+            x_tile = x_rows[b, r // (CHANNEL_TILES // 2)][:, r % (CHANNEL_TILES // 2), :]
+            if b < BATCH - 1:
+                nc.gpsimd.tensor_scalar(
+                    out=result[:], in0=x_tile, scalar1=1.0, scalar2=shift[:, r : r + 1], op0=ALU.mult, op1=ALU.add
+                )
+            else:
+                nc.scalar.activation(out=result[:], in_=x_tile, func=ACT.Identity, bias=shift[:, r : r + 1])
             results[b, r] = result
 
         def project(b, r):

@@ -87,10 +87,10 @@ def tile_sgcam_pb_kernel(
             aff[0, i] = load_affinity(0, i)
         w_rows = loads.tile([P, CHANNEL_TILES, INNER], BF16)
         nc.sync.dma_start(out=w_rows[:], in_=w_w.rearrange("(p r) k -> p r k", r=CHANNEL_TILES))
-        for g in range(SOURCE_PASSES):
-            gx_raw[1, g] = load_values(1, g)
         for h in range(2):
             x_rows[0, h] = load_residual(0, h)
+        for g in range(SOURCE_PASSES):
+            gx_raw[1, g] = load_values(1, g)
         for i in range(CHUNKS):
             aff[1, i] = load_affinity(1, i)
         for h in range(2):
@@ -218,10 +218,10 @@ def tile_sgcam_pb_kernel(
 
         results = {}
 
-        def shift_residual(b, r):
+        def shift_residual(b, r, on_gpsimd=False):
             result = keep.tile([P, POINTS], F32, name="result%d%d" % (b, r))
             x_tile = x_rows[b, r // (CHANNEL_TILES // 2)][:, r % (CHANNEL_TILES // 2), :]
-            if b < BATCH - 1:
+            if on_gpsimd:
                 nc.gpsimd.tensor_scalar(
                     out=result[:], in0=x_tile, scalar1=1.0, scalar2=shift[:, r : r + 1], op0=ALU.mult, op1=ALU.add
                 )
@@ -232,6 +232,8 @@ def tile_sgcam_pb_kernel(
         def project(b, r):
             chans = slice(r * P, (r + 1) * P)
             result = results[b, r]
+            out_tile = out[b].rearrange("(p r) n -> p r n", r=CHANNEL_TILES)[:, r, :]
+            last_tile = b == BATCH - 1 and r == CHANNEL_TILES - 1
             for h in range(HALVES):
                 acc = banks.tile([P, HALF], F32, name="acc", tag="bank")
                 nc.tensor.matmul_mx(
@@ -252,7 +254,10 @@ def tile_sgcam_pb_kernel(
                     op0=ALU.mult,
                     op1=ALU.add,
                 )
-            nc.sync.dma_start(out=out[b].rearrange("(p r) n -> p r n", r=CHANNEL_TILES)[:, r, :], in_=result[:])
+                if last_tile:
+                    nc.sync.dma_start(out=out_tile[:, pts], in_=result[:, pts])
+            if not last_tile:
+                nc.sync.dma_start(out=out_tile, in_=result[:])
 
         AHEAD = 2
         start_batch_norm()
@@ -280,10 +285,16 @@ def tile_sgcam_pb_kernel(
                 aggregate(b, i)
                 if i == CHUNKS - 2:
                     quantise_y(b, 0)
-            for r in range(CHANNEL_TILES):
-                shift_residual(b, r)
-            if b == 0:
+                if b > 0 and i < CHUNKS // 2:
+                    shift_residual(b - 1, CHANNEL_TILES // 2 + 2 * i)
+                    shift_residual(b - 1, CHANNEL_TILES // 2 + 2 * i + 1)
+            if b < BATCH - 1:
+                for r in range(CHANNEL_TILES // 2):
+                    shift_residual(b, r, on_gpsimd=True)
                 quantise_weights()
+            else:
+                for r in range(CHANNEL_TILES):
+                    shift_residual(b, r)
         quantise_y(BATCH - 1, HALVES - 1)
         for r in range(CHANNEL_TILES):
             project(BATCH - 1, r)

from contextlib import ExitStack

import concourse.masks as masks
import concourse.mybir as mybir

F32 = mybir.dt.float32
BF16 = mybir.dt.bfloat16
U32 = mybir.dt.uint32
U8 = mybir.dt.uint8
FP8X4 = mybir.dt.float8_e4m3fn_x4
ALU = mybir.AluOpType
ACT = mybir.ActivationFunctionType

P = 128
PACK = 4
K_PASS = P * PACK

BATCH = 2
POINTS = 1024
INNER = 512
CHANNELS = 1024
EPS = 1e-5

SOURCE_PASSES = POINTS // K_PASS
INNER_TILES = INNER // P
CHANNEL_TILES = CHANNELS // P
CHUNK = 2 * P
CHUNKS = POINTS // CHUNK
HALF = 512
HALVES = POINTS // HALF

FLOPS = 2 * BATCH * POINTS * POINTS * INNER + 2 * BATCH * CHANNELS * INNER * POINTS


def tile_sgcam_pb_kernel(
    tc, affinity, g_x, w_w, w_b, bn_gamma, bn_beta, bn_mean, bn_var, x, out
):
    nc = tc.nc
    with ExitStack() as ctx:
        const = ctx.enter_context(tc.tile_pool(name="const", bufs=1))
        loads = ctx.enter_context(tc.tile_pool(name="loads", bufs=1))
        keep = ctx.enter_context(tc.tile_pool(name="keep", bufs=1))
        stage = ctx.enter_context(tc.tile_pool(name="stage", bufs=2))
        chunk_pool = ctx.enter_context(tc.tile_pool(name="chunk", bufs=4))
        banks = ctx.enter_context(tc.psum_pool(name="banks", bufs=8))
        ctx.enter_context(tc.manual_schedule())

        def load_values(b, g):
            raw = loads.tile([P, PACK, INNER], BF16, name="gx_raw%d%d" % (b, g))
            nc.sync.dma_start(
                out=raw[:].rearrange("q (u e) c -> q u (e c)", e=2),
                in_=g_x[b, g * K_PASS : (g + 1) * K_PASS, :].rearrange("(u q e) c -> q u (e c)", u=2, e=2),
            )
            return raw

        def load_affinity(b, i):
            rows = loads.tile([P, 2, POINTS], BF16, name="aff%d%d" % (b, i))
            nc.sync.dma_start(
                out=rows[:],
                in_=affinity[b, i * CHUNK : (i + 1) * CHUNK, :].rearrange("(p j) m -> p j m", j=2),
            )
            return rows

        def load_residual(b, h):
            rows = loads.tile([P, CHANNEL_TILES // 2, POINTS], BF16, name="x%d%d" % (b, h))
            half_rows = slice(h * CHANNEL_TILES // 2, (h + 1) * CHANNEL_TILES // 2)
            nc.sync.dma_start(out=rows[:], in_=x[b].rearrange("(p r) n -> p r n", r=CHANNEL_TILES)[:, half_rows, :])
            return rows

        def load_vector(vec, name):
            rows = const.tile([P, CHANNEL_TILES], BF16, name=name)
            nc.scalar.dma_start(out=rows[:], in_=vec.rearrange("(p r) -> p r", r=CHANNEL_TILES))
            return rows

        var_bf = load_vector(bn_var, "var_bf")
        gamma_bf = load_vector(bn_gamma, "gamma_bf")
        bias_bf = load_vector(w_b, "bias_bf")
        mean_bf = load_vector(bn_mean, "mean_bf")
        beta_bf = load_vector(bn_beta, "beta_bf")

        gx_raw = {}
        aff = {}
        x_rows = {}
        for g in range(SOURCE_PASSES):
            gx_raw[0, g] = load_values(0, g)
        for i in range(CHUNKS):
            aff[0, i] = load_affinity(0, i)
        w_rows = loads.tile([P, CHANNEL_TILES, INNER], BF16)
        nc.sync.dma_start(out=w_rows[:], in_=w_w.rearrange("(p r) k -> p r k", r=CHANNEL_TILES))
        for h in range(2):
            x_rows[0, h] = load_residual(0, h)
        for g in range(SOURCE_PASSES):
            gx_raw[1, g] = load_values(1, g)
        for i in range(CHUNKS):
            aff[1, i] = load_affinity(1, i)
        for h in range(2):
            x_rows[1, h] = load_residual(1, h)

        ident_f32 = const.tile([P, P], F32)
        masks.make_identity(nc, ident_f32[:])
        ident_bf = const.tile([P, P], BF16)
        masks.make_identity(nc, ident_bf[:])

        gx_grouped = {}
        gx_codes = {}
        gx_scales = {}

        def regroup_values(b, g):
            grouped = stage.tile([P, INNER, PACK], BF16, name="gx_grouped", align_bytes=64)
            regroup = nc.vector.tensor_copy if g == 0 else nc.scalar.copy
            regroup(
                out=grouped[:].rearrange("q (c i) t -> q c t i", i=4),
                in_=gx_raw[b, g][:].rearrange("q t (c i) -> q c t i", i=4),
            )
            gx_grouped[b, g] = grouped

        def quantise_values(b, g):
            codes = keep.tile([P, INNER], U32, name="gx_codes%d%d" % (b, g), align_bytes=64)
            scales = keep.tile([P, INNER], U8, name="gx_scales%d%d" % (b, g), align_bytes=64)
            nc.vector.quantize_mx(
                out=codes[:].bitcast(FP8X4), scales=scales[:], in_=gx_grouped[b, g][:].rearrange("q c t -> q (c t)")
            )
            gx_codes[b, g] = codes
            gx_scales[b, g] = scales

        aff_grouped = {}
        aff_codes = {}
        aff_scales = {}

        def flip_affinity(b, i):
            words = aff[b, i][:].rearrange("p j m -> p (j m)").bitcast(F32)
            grouped = chunk_pool.tile([P, SOURCE_PASSES * CHUNK * PACK], BF16, name="aff_grouped", align_bytes=64)
            grouped_words = grouped[:].bitcast(F32).rearrange(
                "q (g p j u) -> q g p j u", g=SOURCE_PASSES, j=2, u=2
            )
            for g in range(SOURCE_PASSES):
                flipped = banks.tile([P, 2, 2, P], F32, name="flipped", tag="bank")
                for j in range(2):
                    for u in range(2):
                        first = j * (POINTS // 2) + g * (K_PASS // 2) + u * P
                        nc.tensor.transpose(flipped[:, j, u, :], words[:, first : first + P], ident_f32[:])
                nc.scalar.copy(out=grouped_words[:, g], in_=flipped[:].rearrange("q j u p -> q p j u"))
            aff_grouped[b, i] = grouped

        def quantise_affinity(b, i):
            codes = chunk_pool.tile([P, SOURCE_PASSES * CHUNK], U32, name="aff_codes", align_bytes=64)
            scales = chunk_pool.tile([P, SOURCE_PASSES * CHUNK], U8, name="aff_scales", align_bytes=64)
            nc.vector.quantize_mx(out=codes[:].bitcast(FP8X4), scales=scales[:], in_=aff_grouped[b, i][:])
            aff_codes[b, i] = codes
            aff_scales[b, i] = scales

        y_grouped = {}
        y_codes = {}
        y_scales = {}

        def aggregate(b, i):
            h, k = divmod(i, HALF // CHUNK)
            if k == 0:
                y_grouped[b, h] = stage.tile([P, HALF, PACK], BF16, name="y_grouped", align_bytes=64)
            for s in range(CHUNK // P):
                y_bank = banks.tile([P, INNER_TILES, P], F32, name="y_bank", tag="bank")
                for t in range(INNER_TILES):
                    for g in range(SOURCE_PASSES):
                        ci = slice(t * P, (t + 1) * P)
                        pts = slice(g * CHUNK + s * P, g * CHUNK + (s + 1) * P)
                        nc.tensor.matmul_mx(
                            out=y_bank[:, t, :],
                            lhsT=gx_codes[b, g][:, ci].bitcast(FP8X4),
                            lhsT_scale=gx_scales[b, g][:, ci],
                            rhs=aff_codes[b, i][:, pts].bitcast(FP8X4),
                            rhs_scale=aff_scales[b, i][:, pts],
                            start=(g == 0),
                            stop=(g == SOURCE_PASSES - 1),
                        )
                lo = k * CHUNK + s * P
                nc.scalar.copy(out=y_grouped[b, h][:, lo : lo + P, :], in_=y_bank[:].rearrange("q t n -> q n t"))

        def quantise_y(b, h):
            codes = keep.tile([P, HALF], U32, name="y_codes%d%d" % (b, h), align_bytes=64)
            scales = keep.tile([P, HALF], U8, name="y_scales%d%d" % (b, h), align_bytes=64)
            nc.vector.quantize_mx(
                out=codes[:].bitcast(FP8X4), scales=scales[:], in_=y_grouped[b, h][:].rearrange("q n t -> q (n t)")
            )
            y_codes[b, h] = codes
            y_scales[b, h] = scales

        w_grouped = keep.tile([P, CHANNEL_TILES, P, PACK], BF16, align_bytes=64)
        w_codes = keep.tile([P, CHANNELS], U32, align_bytes=64)
        w_scales = keep.tile([P, CHANNELS], U8, align_bytes=64)

        def flip_weights(pair):
            flipped = banks.tile([P, 2, INNER_TILES, P], BF16, name="w_flipped", tag="bank")
            for k in range(2):
                for t in range(INNER_TILES):
                    nc.tensor.transpose(flipped[:, k, t, :], w_rows[:, 2 * pair + k, t * P : (t + 1) * P], ident_bf[:])
            copy_out = nc.scalar.copy if pair % 2 == 0 else nc.vector.tensor_copy
            copy_out(out=w_grouped[:, 2 * pair : 2 * pair + 2, :, :], in_=flipped[:].rearrange("q k t p -> q k p t"))

        def quantise_weights():
            nc.vector.quantize_mx(
                out=w_codes[:].bitcast(FP8X4), scales=w_scales[:], in_=w_grouped[:].rearrange("q r p t -> q (r p t)")
            )

        std = const.tile([P, CHANNEL_TILES], F32)
        gain = const.tile([P, CHANNEL_TILES], F32)
        shift = const.tile([P, CHANNEL_TILES], F32)

        def start_batch_norm():
            nc.vector.tensor_scalar_add(out=std[:], in0=var_bf[:], scalar1=EPS)
            nc.scalar.sqrt(out=std[:], in_=std[:])

        def finish_batch_norm():
            nc.vector.reciprocal(out=gain[:], in_=std[:])
            nc.vector.tensor_mul(out=gain[:], in0=gain[:], in1=gamma_bf[:])
            nc.vector.tensor_sub(out=shift[:], in0=bias_bf[:], in1=mean_bf[:])
            nc.vector.tensor_mul(out=shift[:], in0=shift[:], in1=gain[:])
            nc.vector.tensor_add(out=shift[:], in0=shift[:], in1=beta_bf[:])

        results = {}

        def shift_residual(b, r, on_gpsimd=False):
            result = keep.tile([P, POINTS], F32, name="result%d%d" % (b, r))
            x_tile = x_rows[b, r // (CHANNEL_TILES // 2)][:, r % (CHANNEL_TILES // 2), :]
            if on_gpsimd:
                nc.gpsimd.tensor_scalar(
                    out=result[:], in0=x_tile, scalar1=1.0, scalar2=shift[:, r : r + 1], op0=ALU.mult, op1=ALU.add
                )
            else:
                nc.scalar.activation(out=result[:], in_=x_tile, func=ACT.Identity, bias=shift[:, r : r + 1])
            results[b, r] = result

        def project(b, r):
            chans = slice(r * P, (r + 1) * P)
            result = results[b, r]
            out_tile = out[b].rearrange("(p r) n -> p r n", r=CHANNEL_TILES)[:, r, :]
            last_tile = b == BATCH - 1 and r == CHANNEL_TILES - 1
            for h in range(HALVES):
                acc = banks.tile([P, HALF], F32, name="acc", tag="bank")
                nc.tensor.matmul_mx(
                    out=acc[:],
                    lhsT=w_codes[:, chans].bitcast(FP8X4),
                    lhsT_scale=w_scales[:, chans],
                    rhs=y_codes[b, h][:].bitcast(FP8X4),
                    rhs_scale=y_scales[b, h][:],
                    start=True,
                    stop=True,
                )
                pts = slice(h * HALF, (h + 1) * HALF)
                nc.vector.scalar_tensor_tensor(
                    out=result[:, pts],
                    in0=acc[:],
                    scalar=gain[:, r : r + 1],
                    in1=result[:, pts],
                    op0=ALU.mult,
                    op1=ALU.add,
                )
                if last_tile:
                    nc.sync.dma_start(out=out_tile[:, pts], in_=result[:, pts])
            if not last_tile:
                nc.sync.dma_start(out=out_tile, in_=result[:])

        AHEAD = 2
        start_batch_norm()
        for b in range(BATCH):
            for g in range(SOURCE_PASSES):
                regroup_values(b, g)
            if b == 0:
                finish_batch_norm()
            else:
                quantise_y(b - 1, HALVES - 1)
            for g in range(SOURCE_PASSES):
                quantise_values(b, g)
            for i in range(AHEAD):
                flip_affinity(b, i)
            for i in range(CHUNKS):
                quantise_affinity(b, i)
                if b > 0:
                    project(b - 1, 2 * i)
                    project(b - 1, 2 * i + 1)
                if i + AHEAD < CHUNKS:
                    flip_affinity(b, i + AHEAD)
                elif b == 0:
                    flip_weights(2 * (i + AHEAD - CHUNKS))
                    flip_weights(2 * (i + AHEAD - CHUNKS) + 1)
                aggregate(b, i)
                if i == CHUNKS - 2:
                    quantise_y(b, 0)
                if b > 0 and i < CHUNKS // 2:
                    shift_residual(b - 1, CHANNEL_TILES // 2 + 2 * i)
                    shift_residual(b - 1, CHANNEL_TILES // 2 + 2 * i + 1)
            if b < BATCH - 1:
                for r in range(CHANNEL_TILES // 2):
                    shift_residual(b, r, on_gpsimd=True)
                quantise_weights()
            else:
                for r in range(CHANNEL_TILES):
                    shift_residual(b, r)
        quantise_y(BATCH - 1, HALVES - 1)
        for r in range(CHANNEL_TILES):
            project(BATCH - 1, r)
